import numpy as np
import ml_dtypes


BF16 = ml_dtypes.bfloat16


def bf(x):
    return np.asarray(x, np.float32).astype(BF16)


def f64(x):
    return np.asarray(x).astype(np.float64)


E2M1 = np.array([0.0, 0.5, 1.0, 1.5, 2.0, 3.0, 4.0, 6.0, -0.0, -0.5, -1.0, -1.5, -2.0, -3.0, -4.0, -6.0])


def pack_weight(w, fmt):
    k, n = w.shape
    w = f64(bf(w)).reshape(k // 32, 32, n)
    amax = np.abs(w).max(1)
    if fmt == "e4m3":
        byte = np.frexp(amax)[1] - 1 + 127 - 7
    else:
        mant, ex = np.frexp(amax / 6.0)
        byte = np.where(mant > 0.5, ex, ex - 1) + 127
    byte = np.clip(np.where(amax > 0, byte, 1), 1, 254)
    scaled = (w * np.exp2(127.0 - byte)[:, None, :]).reshape(k, n).astype(np.float32)
    by_word = np.ascontiguousarray(scaled.reshape(k // 512, 128, 4, n).transpose(0, 1, 3, 2))
    if fmt == "e4m3":
        words = by_word.astype(ml_dtypes.float8_e4m3fn).view(np.uint8)
    else:
        c = by_word.astype(ml_dtypes.float4_e2m1fn).view(np.uint8) & 0xF
        words = c[..., 0::2] | (c[..., 1::2] << 4)
    return np.ascontiguousarray(words), np.ascontiguousarray(byte.astype(np.uint8).reshape(k // 512, 16, n))


def unpack_weight(words, scales, fmt):
    g, p, n, _ = words.shape
    if fmt == "e4m3":
        vals = np.ascontiguousarray(words).view(ml_dtypes.float8_e4m3fn).astype(np.float64)
    else:
        nib = np.empty((g, p, n, 4), np.uint8)
        nib[..., 0::2] = words & 0xF
        nib[..., 1::2] = words >> 4
        vals = E2M1[nib]
    vals = vals * np.repeat(np.exp2(scales.astype(np.float64) - 127.0), 8, axis=1)[..., None]
    return vals.transpose(0, 1, 3, 2).reshape(g * 512, n)

def pack4(w):
    words, scales = pack_weight(w, "e2m1")
    return words.reshape(words.shape[0], 128, -1), scales


def unpack4(words, scales):
    return unpack_weight(words.reshape(words.shape[0], 128, -1, 2), scales, "e2m1")


def kspread(k):
    return np.exp2(np.repeat(np.random.randint(-6, 7, k // 32), 32).astype(np.float64))


B, S, D, H, DH, QB = 1, 2048, 4096, 8, 128, 512
HD = H * DH
ROPE_BASE = 10000.0


def rope(t):
    b, h, s, d = t.shape
    inv_freq = 1.0 / (ROPE_BASE ** (np.arange(0, d, 2) / d))
    ang = np.arange(s)[:, None] * inv_freq[None, :]
    cos = np.cos(ang)[None, None]
    sin = np.sin(ang)[None, None]
    t1 = t[..., 0::2]
    t2 = t[..., 1::2]
    r1 = t1 * cos - t2 * sin
    r2 = t1 * sin + t2 * cos
    return np.stack([r1, r2], axis=-1).reshape(b, h, s, d)


def setup_inputs():
    s = kspread(D)
    x = np.random.standard_normal((B, S, D)) * s
    wq = np.random.standard_normal((HD, D)) / np.sqrt(D) / s[None, :]
    wk = np.random.standard_normal((HD, D)) / np.sqrt(D) / s[None, :]
    x_words, x_scales = pack4(x.reshape(B * S, D).T)
    wq_words, wq_scales = pack4(wq.T)
    wk_words, wk_scales = pack4(wk.T)
    return {"x_words": x_words, "x_scales": x_scales,
            "wq_words": wq_words, "wq_scales": wq_scales,
            "wk_words": wk_words, "wk_scales": wk_scales}


def reference(x_words, x_scales, wq_words, wq_scales, wk_words, wk_scales):
    xq = unpack4(x_words, x_scales).T.reshape(B, S, D)
    q = (xq @ unpack4(wq_words, wq_scales)).reshape(B, S, H, DH).transpose(0, 2, 1, 3)
    k = (xq @ unpack4(wk_words, wk_scales)).reshape(B, S, H, DH).transpose(0, 2, 1, 3)
    return np.maximum(rope(q), 0.0), np.maximum(rope(k), 0.0)

@@ -1,0 +1,229 @@
+from contextlib import ExitStack
+
+import concourse.mybir as mybir
+
+FLOPS = 2 * 2048 * 4096 * 2048
+
+F32 = mybir.dt.float32
+I32 = mybir.dt.int32
+U8 = mybir.dt.uint8
+FP4X4 = mybir.dt.float4_e2m1fn_x4
+ALU = mybir.AluOpType
+ACTF = mybir.ActivationFunctionType
+
+P = 128
+PASSES = 8
+N_TILE = 512
+TOKEN_TILES = 16
+PAIRS = 64
+DH = 128
+TWO_PI = 6.283185307179586
+ROPE_BASE = 10000.0
+SPLIT_PAIRS = 32
+HI_BITS = 13
+BANKS = 8
+
+
+def split_hi_lo(value):
+    shift = 0
+    while value * 2.0**shift < 2.0 ** (HI_BITS - 1):
+        shift += 1
+    hi = round(value * 2.0**shift) / 2.0**shift
+    return hi, value - hi
+
+
+def tile_linearattention_pa_kernel(
+    tc, x_words, x_scales, wq_words, wq_scales, wk_words, wk_scales, out_0, out_1
+):
+    nc = tc.nc
+    parts = {
+        "x0": (x_words, x_scales, 0, 512),
+        "x1": (x_words, x_scales, 512, 1024),
+        "x2": (x_words, x_scales, 1024, 1536),
+        "x3": (x_words, x_scales, 1536, 2048),
+        "wq": (wq_words, wq_scales, 0, 1024),
+        "wk": (wk_words, wk_scales, 0, 1024),
+    }
+
+    with ExitStack() as ctx:
+        keep = ctx.enter_context(tc.tile_pool(name="keep", bufs=1))
+        ep = ctx.enter_context(tc.tile_pool(name="ep", bufs=4))
+        psum = ctx.enter_context(tc.psum_pool(name="psum", bufs=BANKS))
+        ctx.enter_context(tc.manual_schedule())
+
+        codes = {}
+        planes = {}
+
+        def make_planes(name, g0, g1):
+            c0, c1 = parts[name][2], parts[name][3]
+            t = keep.tile([P, g1 - g0, c1 - c0], U8, name="%s_p%d" % (name, g0), align_bytes=64)
+            nc.vector.memset(t[:].bitcast(I32), 0)
+            for g in range(g0, g1):
+                planes[(name, g)] = (t, g - g0)
+
+        def load_scales(name, g0, g1):
+            scales, c0, c1 = parts[name][1], parts[name][2], parts[name][3]
+            t = planes[(name, g0)][0]
+            for q in range(4):
+                nc.sync.dma_start(
+                    out=t[32 * q : 32 * q + 4, :, :].bitcast(I32),
+                    in_=scales[g0:g1, 4 * q : 4 * q + 4, c0:c1].rearrange("g r n -> r g n").bitcast(I32),
+                )
+
+        def load_codes(name, g0, g1):
+            words, c0, c1 = parts[name][0], parts[name][2], parts[name][3]
+            t = keep.tile([P, g1 - g0, 2 * (c1 - c0)], U8, name="%s_c%d" % (name, g0), align_bytes=64)
+            nc.sync.dma_start(
+                out=t[:].bitcast(I32),
+                in_=words[g0:g1, :, 2 * c0 : 2 * c1].rearrange("g p n -> p g n").bitcast(I32),
+            )
+            for g in range(g0, g1):
+                codes[(name, g)] = (t, g - g0)
+
+        pos = keep.tile([P, TOKEN_TILES], F32, name="pos")
+        nc.gpsimd.iota(pos[:], pattern=[[P, TOKEN_TILES]], base=0, channel_multiplier=1, allow_small_or_imprecise_dtypes=True)
+
+        make_planes("x0", 0, 1)
+        make_planes("wq", 0, 1)
+        make_planes("x0", 1, 8)
+        make_planes("wq", 1, 4)
+        make_planes("wq", 4, 8)
+
+        load_scales("x0", 0, 1)
+        load_scales("wq", 0, 1)
+        load_codes("x0", 0, 1)
+        load_codes("wq", 0, 1)
+        load_scales("x0", 1, 8)
+        load_scales("wq", 1, 4)
+        for g in range(1, 4):
+            load_codes("x0", g, g + 1)
+            load_codes("wq", g, g + 1)
+        load_scales("wq", 4, 8)
+        for g in range(4, 8):
+            load_codes("x0", g, g + 1)
+            load_codes("wq", g, g + 1)
+
+        warm = keep.tile([P, 1], F32, name="warm")
+        nc.scalar.activation(out=warm[:], in_=pos[:, 0:1], func=ACTF.Sin, scale=0.0)
+        t1 = keep.tile([P, TOKEN_TILES, PAIRS], F32, name="t1")
+        t2 = keep.tile([P, TOKEN_TILES, SPLIT_PAIRS], F32, name="t2")
+        for j in range(PAIRS):
+            turns = ROPE_BASE ** (-j / 64.0) / TWO_PI
+            if j < SPLIT_PAIRS:
+                hi, lo = split_hi_lo(turns)
+                nc.vector.tensor_scalar(out=t1[:, :, j], in0=pos[:], scalar1=hi, scalar2=None, op0=ALU.mult)
+                nc.scalar.activation(out=t2[:, :, j], in_=pos[:], func=ACTF.Copy, scale=lo)
+            else:
+                nc.scalar.activation(out=t1[:, :, j], in_=pos[:], func=ACTF.Copy, scale=turns)
+
+        make_planes("x1", 0, 8)
+        make_planes("wk", 0, 8)
+        load_scales("x1", 0, 8)
+        load_codes("x1", 0, 4)
+        load_codes("x1", 4, 8)
+        load_scales("wk", 0, 8)
+        for g in range(0, 8, 2):
+            load_codes("wk", g, g + 2)
+
+        whole = keep.tile([P, TOKEN_TILES, PAIRS], I32, name="whole")
+        frac = keep.tile([P, TOKEN_TILES, PAIRS], F32, name="frac")
+        z1 = keep.tile([P, TOKEN_TILES, PAIRS], F32, name="z1")
+        zs = keep.tile([P, TOKEN_TILES, PAIRS], F32, name="zs")
+        gq = keep.tile([P, TOKEN_TILES, PAIRS], F32, name="gq")
+        zc = keep.tile([P, TOKEN_TILES, PAIRS], F32, name="zc")
+        sin_t = keep.tile([P, TOKEN_TILES, PAIRS], F32, name="sin_t")
+        cos_t = keep.tile([P, TOKEN_TILES, PAIRS], F32, name="cos_t")
+        nc.vector.tensor_copy(out=whole[:], in_=t1[:])
+        nc.vector.tensor_tensor(out=frac[:], in0=t1[:], in1=whole[:], op=ALU.subtract)
+        nc.vector.tensor_tensor(out=frac[:, :, 0:SPLIT_PAIRS], in0=frac[:, :, 0:SPLIT_PAIRS], in1=t2[:], op=ALU.add)
+        nc.vector.scalar_tensor_tensor(out=z1[:], in0=frac[:], scalar=0.5, in1=frac[:], op0=ALU.is_gt, op1=ALU.subtract)
+        nc.vector.tensor_scalar(out=gq[:], in0=frac[:], scalar1=0.25, scalar2=None, op0=ALU.add)
+        nc.vector.scalar_tensor_tensor(out=zs[:], in0=z1[:], scalar=0.5, in1=z1[:], op0=ALU.is_gt, op1=ALU.subtract)
+        nc.vector.scalar_tensor_tensor(out=zc[:], in0=gq[:], scalar=0.5, in1=gq[:], op0=ALU.is_gt, op1=ALU.subtract)
+        nc.scalar.activation(out=sin_t[:], in_=zs[:], func=ACTF.Sin, scale=TWO_PI)
+        nc.scalar.activation(out=cos_t[:], in_=zc[:], func=ACTF.Sin, scale=-TWO_PI)
+        make_planes("x2", 0, 8)
+        make_planes("x3", 0, 8)
+
+        def one_pass(acc, unit, g):
+            t, wn, c0, n = unit
+            xn = "x%d" % (t // 4)
+            tl = t % 4
+            xc, xci = codes[(xn, g)]
+            wc, wci = codes[(wn, g)]
+            xp, xpi = planes[(xn, g)]
+            wp, wpi = planes[(wn, g)]
+            nc.tensor.matmul_mx(
+                out=acc[:],
+                lhsT=xc[:, xci, 2 * P * tl : 2 * P * (tl + 1)].bitcast(FP4X4),
+                lhsT_scale=xp[:, xpi, P * tl : P * (tl + 1)],
+                rhs=wc[:, wci, 2 * c0 : 2 * (c0 + n)].bitcast(FP4X4),
+                rhs_scale=wp[:, wpi, c0 : c0 + n],
+                start=(g == 0),
+                stop=(g == PASSES - 1),
+            )
+
+        held = {}
+
+        def multiply(i):
+            t, wn, c0, n = units[i]
+            shape = [P, 2, n // DH, PAIRS]
+            u = accs[i][:].rearrange("p (h j e) -> p e h j", h=n // DH, j=PAIRS, e=2)
+            uc = ep.tile(shape, F32, name="uc")
+            us = ep.tile(shape, F32, name="us")
+            nc.vector.tensor_tensor(out=uc[:], in0=u, in1=cos_t[:, t, :].unsqueeze(1).unsqueeze(1).to_broadcast(shape), op=ALU.mult)
+            nc.vector.tensor_tensor(out=us[:], in0=u, in1=sin_t[:, t, :].unsqueeze(1).unsqueeze(1).to_broadcast(shape), op=ALU.mult)
+            held[i] = (uc, us)
+
+        def finish(i):
+            t, wn, c0, n = units[i]
+            nh = n // DH
+            uc, us = held[i]
+            rot = ep.tile([P, 2, nh, PAIRS], F32, name="rot")
+            res = ep.tile([P, nh, PAIRS, 2], F32, name="res", bufs=6)
+            nc.vector.tensor_tensor(out=rot[:, 0], in0=uc[:, 0], in1=us[:, 1], op=ALU.subtract)
+            nc.vector.tensor_tensor(out=rot[:, 1], in0=uc[:, 1], in1=us[:, 0], op=ALU.add)
+            nc.scalar.activation(out=res[:], in_=rot[:].rearrange("p e h j -> p h j e"), func=ACTF.Relu)
+            dst = out_0 if wn == "wq" else out_1
+            h0 = c0 // DH
+            nc.sync.dma_start(
+                out=dst[0, h0 : h0 + nh, P * t : P * (t + 1), :].rearrange("h p d -> p h d"),
+                in_=res[:].rearrange("p h j e -> p h (j e)"),
+            )
+
+        units = [(t, "wq", c0, N_TILE) for t in range(0, 8) for c0 in (0, 512)]
+        units += [(t, "wk", c0, N_TILE) for t in range(0, 8) for c0 in (0, 512)]
+        units += [(t, wn, c0, N_TILE) for t in range(8, TOKEN_TILES) for wn in ("wq", "wk") for c0 in (0, 512)]
+        last = units.pop()
+        units += [(last[0], last[1], 512, 256), (last[0], last[1], 768, 128), (last[0], last[1], 896, 128)]
+
+        accs = []
+        for i in range(BANKS):
+            acc = psum.tile([P, N_TILE], F32, name="acc")
+            accs.append(acc)
+        for g in range(PASSES):
+            for i in range(BANKS):
+                one_pass(accs[i], units[i], g)
+        for i in range(BANKS, len(units)):
+            multiply(i - BANKS)
+            if i > BANKS:
+                finish(i - BANKS - 1)
+            if i == 16:
+                load_scales("x2", 0, 8)
+                load_codes("x2", 0, 4)
+                load_codes("x2", 4, 8)
+            if i == 32:
+                load_scales("x3", 0, 8)
+                load_codes("x3", 0, 4)
+                load_codes("x3", 4, 8)
+            acc = psum.tile([P, units[i][3]], F32, name="acc")
+            accs.append(acc)
+            for g in range(PASSES):
+                one_pass(acc, units[i], g)
+        for i in range(len(units) - BANKS, len(units) - 3):
+            multiply(i)
+            finish(i - 1)
+        finish(len(units) - 4)
+        for i in range(len(units) - 3, len(units)):
+            multiply(i)
+            finish(i)

@@ -7,6 +7,7 @@ FLOPS = 2 * 2048 * 4096 * 2048
 F32 = mybir.dt.float32
 I32 = mybir.dt.int32
 U8 = mybir.dt.uint8
+BF16 = mybir.dt.bfloat16
 FP4X4 = mybir.dt.float4_e2m1fn_x4
 ALU = mybir.AluOpType
 ACTF = mybir.ActivationFunctionType
@@ -22,6 +23,8 @@ ROPE_BASE = 10000.0
 SPLIT_PAIRS = 32
 HI_BITS = 13
 BANKS = 8
+WARM_MATMULS = 12
+LAG_UNTIL = 40
 
 
 def split_hi_lo(value):
@@ -85,6 +88,8 @@ def tile_linearattention_pa_kernel(
 
         make_planes("x0", 0, 1)
         make_planes("wq", 0, 1)
+        zz = keep.tile([P, N_TILE], BF16, name="zz")
+        nc.vector.memset(zz[:], 0.0)
         make_planes("x0", 1, 8)
         make_planes("wq", 1, 4)
         make_planes("wq", 4, 8)
@@ -131,7 +136,7 @@ def tile_linearattention_pa_kernel(
         zs = keep.tile([P, TOKEN_TILES, PAIRS], F32, name="zs")
         gq = keep.tile([P, TOKEN_TILES, PAIRS], F32, name="gq")
         zc = keep.tile([P, TOKEN_TILES, PAIRS], F32, name="zc")
-        sin_t = keep.tile([P, TOKEN_TILES, PAIRS], F32, name="sin_t")
+        sin_t = keep.tile([P, TOKEN_TILES, 2, PAIRS], F32, name="sin_t")
         cos_t = keep.tile([P, TOKEN_TILES, PAIRS], F32, name="cos_t")
         nc.vector.tensor_copy(out=whole[:], in_=t1[:])
         nc.vector.tensor_tensor(out=frac[:], in0=t1[:], in1=whole[:], op=ALU.subtract)
@@ -140,7 +145,8 @@ def tile_linearattention_pa_kernel(
         nc.vector.tensor_scalar(out=gq[:], in0=frac[:], scalar1=0.25, scalar2=None, op0=ALU.add)
         nc.vector.scalar_tensor_tensor(out=zs[:], in0=z1[:], scalar=0.5, in1=z1[:], op0=ALU.is_gt, op1=ALU.subtract)
         nc.vector.scalar_tensor_tensor(out=zc[:], in0=gq[:], scalar=0.5, in1=gq[:], op0=ALU.is_gt, op1=ALU.subtract)
-        nc.scalar.activation(out=sin_t[:], in_=zs[:], func=ACTF.Sin, scale=TWO_PI)
+        nc.scalar.activation(out=sin_t[:, :, 0, :], in_=zs[:], func=ACTF.Sin, scale=TWO_PI)
+        nc.scalar.activation(out=sin_t[:, :, 1, :], in_=zs[:], func=ACTF.Sin, scale=-TWO_PI)
         nc.scalar.activation(out=cos_t[:], in_=zc[:], func=ACTF.Sin, scale=-TWO_PI)
         make_planes("x2", 0, 8)
         make_planes("x3", 0, 8)
@@ -172,17 +178,25 @@ def tile_linearattention_pa_kernel(
             uc = ep.tile(shape, F32, name="uc")
             us = ep.tile(shape, F32, name="us")
             nc.vector.tensor_tensor(out=uc[:], in0=u, in1=cos_t[:, t, :].unsqueeze(1).unsqueeze(1).to_broadcast(shape), op=ALU.mult)
-            nc.vector.tensor_tensor(out=us[:], in0=u, in1=sin_t[:, t, :].unsqueeze(1).unsqueeze(1).to_broadcast(shape), op=ALU.mult)
+            nc.vector.tensor_tensor(out=us[:], in0=u, in1=sin_t[:, t, :, :].unsqueeze(2).to_broadcast(shape), op=ALU.mult)
             held[i] = (uc, us)
 
-        def finish(i):
+        def rotate(i, on_gpsimd):
+            n = units[i][3]
+            uc, us = held[i]
+            rot = ep.tile([P, 2, n // DH, PAIRS], F32, name="rot")
+            if on_gpsimd:
+                nc.gpsimd.tensor_tensor(out=rot[:, 0], in0=uc[:, 0], in1=us[:, 1], op=ALU.add)
+                nc.gpsimd.tensor_tensor(out=rot[:, 1], in0=uc[:, 1], in1=us[:, 0], op=ALU.add)
+            else:
+                nc.vector.tensor_tensor(out=rot[:], in0=uc[:], in1=us[:, ::-1], op=ALU.add)
+            held[i] = rot
+
+        def relu_store(i):
             t, wn, c0, n = units[i]
             nh = n // DH
-            uc, us = held[i]
-            rot = ep.tile([P, 2, nh, PAIRS], F32, name="rot")
+            rot = held[i]
             res = ep.tile([P, nh, PAIRS, 2], F32, name="res", bufs=6)
-            nc.vector.tensor_tensor(out=rot[:, 0], in0=uc[:, 0], in1=us[:, 1], op=ALU.subtract)
-            nc.vector.tensor_tensor(out=rot[:, 1], in0=uc[:, 1], in1=us[:, 0], op=ALU.add)
             nc.scalar.activation(out=res[:], in_=rot[:].rearrange("p e h j -> p h j e"), func=ACTF.Relu)
             dst = out_0 if wn == "wq" else out_1
             h0 = c0 // DH
@@ -195,35 +209,48 @@ def tile_linearattention_pa_kernel(
         units += [(t, "wk", c0, N_TILE) for t in range(0, 8) for c0 in (0, 512)]
         units += [(t, wn, c0, N_TILE) for t in range(8, TOKEN_TILES) for wn in ("wq", "wk") for c0 in (0, 512)]
         last = units.pop()
-        units += [(last[0], last[1], 512, 256), (last[0], last[1], 768, 128), (last[0], last[1], 896, 128)]
+        units += [(last[0], last[1], c0, 256) for c0 in (512, 768)]
+        n_units = len(units)
+
+        steps = []
+        for k in range(LAG_UNTIL):
+            steps.append(("M", k))
+            if k > 0:
+                steps += [("R", k - 1), ("A", k - 1)]
+        steps += [("R", LAG_UNTIL - 1), ("A", LAG_UNTIL - 1)]
+        for k in range(LAG_UNTIL, n_units - 4):
+            steps += [("M", k), ("R", k), ("A", k)]
+        a = n_units - 4
+        steps += [("M", a), ("G", a), ("A", a), ("M", a + 1), ("G", a + 1)]
+        steps += [("M", a + 2), ("R", a + 2), ("A", a + 2), ("A", a + 1), ("M", a + 3), ("R", a + 3), ("A", a + 3)]
 
         accs = []
         for i in range(BANKS):
             acc = psum.tile([P, N_TILE], F32, name="acc")
             accs.append(acc)
+        for i in range(WARM_MATMULS):
+            nc.tensor.matmul(out=accs[BANKS - 1][:], lhsT=zz[:, 0:P], rhs=zz[:], start=True, stop=True)
         for g in range(PASSES):
             for i in range(BANKS):
                 one_pass(accs[i], units[i], g)
-        for i in range(BANKS, len(units)):
-            multiply(i - BANKS)
-            if i > BANKS:
-                finish(i - BANKS - 1)
-            if i == 16:
-                load_scales("x2", 0, 8)
-                load_codes("x2", 0, 4)
-                load_codes("x2", 4, 8)
-            if i == 32:
-                load_scales("x3", 0, 8)
-                load_codes("x3", 0, 4)
-                load_codes("x3", 4, 8)
-            acc = psum.tile([P, units[i][3]], F32, name="acc")
-            accs.append(acc)
-            for g in range(PASSES):
-                one_pass(acc, units[i], g)
-        for i in range(len(units) - BANKS, len(units) - 3):
-            multiply(i)
-            finish(i - 1)
-        finish(len(units) - 4)
-        for i in range(len(units) - 3, len(units)):
-            multiply(i)
-            finish(i)
+        for kind, k in steps:
+            if kind == "M":
+                multiply(k)
+                i = k + BANKS
+                if i == 16:
+                    load_scales("x2", 0, 8)
+                    load_codes("x2", 0, 4)
+                    load_codes("x2", 4, 8)
+                if i == 32:
+                    load_scales("x3", 0, 8)
+                    load_codes("x3", 0, 4)
+                    load_codes("x3", 4, 8)
+                if i < n_units:
+                    acc = psum.tile([P, units[i][3]], F32, name="acc")
+                    accs.append(acc)
+                    for g in range(PASSES):
+                        one_pass(acc, units[i], g)
+            elif kind == "A":
+                relu_store(k)
+            else:
+                rotate(k, kind == "G")

@@ -86,24 +86,25 @@ def tile_linearattention_pa_kernel(
         pos = keep.tile([P, TOKEN_TILES], F32, name="pos")
         nc.gpsimd.iota(pos[:], pattern=[[P, TOKEN_TILES]], base=0, channel_multiplier=1, allow_small_or_imprecise_dtypes=True)
 
-        make_planes("x0", 0, 1)
-        make_planes("wq", 0, 1)
+        make_planes("x0", 0, 2)
+        make_planes("wq", 0, 2)
         zz = keep.tile([P, N_TILE], BF16, name="zz")
         nc.vector.memset(zz[:], 0.0)
-        make_planes("x0", 1, 8)
-        make_planes("wq", 1, 4)
-        make_planes("wq", 4, 8)
+        make_planes("x0", 2, 8)
+        make_planes("wq", 2, 5)
+        make_planes("wq", 5, 8)
 
-        load_scales("x0", 0, 1)
-        load_scales("wq", 0, 1)
-        load_codes("x0", 0, 1)
-        load_codes("wq", 0, 1)
-        load_scales("x0", 1, 8)
-        load_scales("wq", 1, 4)
-        for g in range(1, 4):
+        load_scales("x0", 0, 2)
+        load_scales("wq", 0, 2)
+        for g in range(0, 2):
             load_codes("x0", g, g + 1)
             load_codes("wq", g, g + 1)
-        load_scales("wq", 4, 8)
+        load_scales("x0", 2, 8)
+        load_scales("wq", 2, 5)
+        for g in range(2, 4):
+            load_codes("x0", g, g + 1)
+            load_codes("wq", g, g + 1)
+        load_scales("wq", 5, 8)
         for g in range(4, 8):
             load_codes("x0", g, g + 1)
             load_codes("wq", g, g + 1)

@@ -59,7 +59,7 @@ def tile_linearattention_pa_kernel(
 
         def make_planes(name, g0, g1):
             c0, c1 = parts[name][2], parts[name][3]
-            t = keep.tile([P, g1 - g0, c1 - c0], U8, name="%s_p%d" % (name, g0), align_bytes=64)
+            t = keep.tile([P, g1 - g0, c1 - c0], U8, name="%s_p%d" % (name, g0), align_bytes=256)
             nc.vector.memset(t[:].bitcast(I32), 0)
             for g in range(g0, g1):
                 planes[(name, g)] = (t, g - g0)
@@ -75,7 +75,7 @@ def tile_linearattention_pa_kernel(
 
         def load_codes(name, g0, g1):
             words, c0, c1 = parts[name][0], parts[name][2], parts[name][3]
-            t = keep.tile([P, g1 - g0, 2 * (c1 - c0)], U8, name="%s_c%d" % (name, g0), align_bytes=64)
+            t = keep.tile([P, g1 - g0, 2 * (c1 - c0)], U8, name="%s_c%d" % (name, g0), align_bytes=256)
             nc.sync.dma_start(
                 out=t[:].bitcast(I32),
                 in_=words[g0:g1, :, 2 * c0 : 2 * c1].rearrange("g p n -> p g n").bitcast(I32),

@@ -23,7 +23,7 @@ ROPE_BASE = 10000.0
 SPLIT_PAIRS = 32
 HI_BITS = 13
 BANKS = 8
-WARM_MATMULS = 12
+WARM_MATMULS = 9
 LAG_UNTIL = 40
 
 

@@ -23,7 +23,7 @@ ROPE_BASE = 10000.0
 SPLIT_PAIRS = 32
 HI_BITS = 13
 BANKS = 8
-WARM_MATMULS = 9
+WARM_MATMULS = 8
 LAG_UNTIL = 40
 
 
@@ -73,15 +73,22 @@ def tile_linearattention_pa_kernel(
                     in_=scales[g0:g1, 4 * q : 4 * q + 4, c0:c1].rearrange("g r n -> r g n").bitcast(I32),
                 )
 
-        def load_codes(name, g0, g1):
-            words, c0, c1 = parts[name][0], parts[name][2], parts[name][3]
-            t = keep.tile([P, g1 - g0, 2 * (c1 - c0)], U8, name="%s_c%d" % (name, g0), align_bytes=256)
+        def load_codes(name, g0, g1, lo=0, hi=None):
+            words, c0 = parts[name][0], parts[name][2]
+            hi = parts[name][3] - c0 if hi is None else hi
+            t = keep.tile([P, g1 - g0, 2 * (hi - lo)], U8, name="%s_c%d_%d" % (name, g0, lo), align_bytes=256)
             nc.sync.dma_start(
                 out=t[:].bitcast(I32),
-                in_=words[g0:g1, :, 2 * c0 : 2 * c1].rearrange("g p n -> p g n").bitcast(I32),
+                in_=words[g0:g1, :, 2 * (c0 + lo) : 2 * (c0 + hi)].rearrange("g p n -> p g n").bitcast(I32),
             )
             for g in range(g0, g1):
-                codes[(name, g)] = (t, g - g0)
+                codes.setdefault((name, g), []).append((t, g - g0, lo, hi))
+
+        def find_codes(name, g, lo, hi):
+            for t, slot, a, b in codes[(name, g)]:
+                if a <= lo and hi <= b:
+                    return t, slot, lo - a
+            return None
 
         pos = keep.tile([P, TOKEN_TILES], F32, name="pos")
         nc.gpsimd.iota(pos[:], pattern=[[P, TOKEN_TILES]], base=0, channel_multiplier=1, allow_small_or_imprecise_dtypes=True)
@@ -94,11 +101,13 @@ def tile_linearattention_pa_kernel(
         make_planes("wq", 2, 5)
         make_planes("wq", 5, 8)
 
+        load_codes("x0", 0, 1)
+        load_codes("wq", 0, 1, 0, 512)
         load_scales("x0", 0, 2)
         load_scales("wq", 0, 2)
-        for g in range(0, 2):
-            load_codes("x0", g, g + 1)
-            load_codes("wq", g, g + 1)
+        load_codes("wq", 0, 1, 512, 1024)
+        load_codes("x0", 1, 2)
+        load_codes("wq", 1, 2)
         load_scales("x0", 2, 8)
         load_scales("wq", 2, 5)
         for g in range(2, 4):
@@ -156,15 +165,15 @@ def tile_linearattention_pa_kernel(
             t, wn, c0, n = unit
             xn = "x%d" % (t // 4)
             tl = t % 4
-            xc, xci = codes[(xn, g)]
-            wc, wci = codes[(wn, g)]
+            xc, xci, xo = find_codes(xn, g, P * tl, P * (tl + 1))
+            wc, wci, wo = find_codes(wn, g, c0, c0 + n)
             xp, xpi = planes[(xn, g)]
             wp, wpi = planes[(wn, g)]
             nc.tensor.matmul_mx(
                 out=acc[:],
-                lhsT=xc[:, xci, 2 * P * tl : 2 * P * (tl + 1)].bitcast(FP4X4),
+                lhsT=xc[:, xci, 2 * xo : 2 * (xo + P)].bitcast(FP4X4),
                 lhsT_scale=xp[:, xpi, P * tl : P * (tl + 1)],
-                rhs=wc[:, wci, 2 * c0 : 2 * (c0 + n)].bitcast(FP4X4),
+                rhs=wc[:, wci, 2 * wo : 2 * (wo + n)].bitcast(FP4X4),
                 rhs_scale=wp[:, wpi, c0 : c0 + n],
                 start=(g == 0),
                 stop=(g == PASSES - 1),
@@ -232,7 +241,7 @@ def tile_linearattention_pa_kernel(
         for i in range(WARM_MATMULS):
             nc.tensor.matmul(out=accs[BANKS - 1][:], lhsT=zz[:, 0:P], rhs=zz[:], start=True, stop=True)
         for g in range(PASSES):
-            for i in range(BANKS):
+            for i in ((0, 2, 4, 6, 1, 3, 5, 7) if g == 0 else range(BANKS)):
                 one_pass(accs[i], units[i], g)
         for kind, k in steps:
             if kind == "M":

@@ -67,7 +67,7 @@ def tile_linearattention_pa_kernel(
         def load_scales(name, g0, g1):
             scales, c0, c1 = parts[name][1], parts[name][2], parts[name][3]
             t = planes[(name, g0)][0]
-            for q in range(4):
+            for q in (0, 2, 1, 3):
                 nc.sync.dma_start(
                     out=t[32 * q : 32 * q + 4, :, :].bitcast(I32),
                     in_=scales[g0:g1, 4 * q : 4 * q + 4, c0:c1].rearrange("g r n -> r g n").bitcast(I32),
@@ -93,8 +93,8 @@ def tile_linearattention_pa_kernel(
         pos = keep.tile([P, TOKEN_TILES], F32, name="pos")
         nc.gpsimd.iota(pos[:], pattern=[[P, TOKEN_TILES]], base=0, channel_multiplier=1, allow_small_or_imprecise_dtypes=True)
 
-        make_planes("x0", 0, 2)
         make_planes("wq", 0, 2)
+        make_planes("x0", 0, 2)
         zz = keep.tile([P, N_TILE], BF16, name="zz")
         nc.vector.memset(zz[:], 0.0)
         make_planes("x0", 2, 8)
@@ -103,8 +103,8 @@ def tile_linearattention_pa_kernel(
 
         load_codes("x0", 0, 1)
         load_codes("wq", 0, 1, 0, 512)
-        load_scales("x0", 0, 2)
         load_scales("wq", 0, 2)
+        load_scales("x0", 0, 2)
         load_codes("wq", 0, 1, 512, 1024)
         load_codes("x0", 1, 2)
         load_codes("wq", 1, 2)

@@ -93,10 +93,10 @@ def tile_linearattention_pa_kernel(
         pos = keep.tile([P, TOKEN_TILES], F32, name="pos")
         nc.gpsimd.iota(pos[:], pattern=[[P, TOKEN_TILES]], base=0, channel_multiplier=1, allow_small_or_imprecise_dtypes=True)
 
-        make_planes("wq", 0, 2)
-        make_planes("x0", 0, 2)
         zz = keep.tile([P, N_TILE], BF16, name="zz")
         nc.vector.memset(zz[:], 0.0)
+        make_planes("wq", 0, 2)
+        make_planes("x0", 0, 2)
         make_planes("x0", 2, 8)
         make_planes("wq", 2, 5)
         make_planes("wq", 5, 8)
@@ -218,8 +218,8 @@ def tile_linearattention_pa_kernel(
         units = [(t, "wq", c0, N_TILE) for t in range(0, 8) for c0 in (0, 512)]
         units += [(t, "wk", c0, N_TILE) for t in range(0, 8) for c0 in (0, 512)]
         units += [(t, wn, c0, N_TILE) for t in range(8, TOKEN_TILES) for wn in ("wq", "wk") for c0 in (0, 512)]
-        last = units.pop()
-        units += [(last[0], last[1], c0, 256) for c0 in (512, 768)]
+        units = units[:-2]
+        units += [(TOKEN_TILES - 1, "wk", c0, n) for c0, n in ((0, 256), (256, 256), (512, 256), (768, 128), (896, 128))]
         n_units = len(units)
 
         steps = []
@@ -228,11 +228,12 @@ def tile_linearattention_pa_kernel(
             if k > 0:
                 steps += [("R", k - 1), ("A", k - 1)]
         steps += [("R", LAG_UNTIL - 1), ("A", LAG_UNTIL - 1)]
-        for k in range(LAG_UNTIL, n_units - 4):
+        for k in range(LAG_UNTIL, n_units - 6):
             steps += [("M", k), ("R", k), ("A", k)]
-        a = n_units - 4
-        steps += [("M", a), ("G", a), ("A", a), ("M", a + 1), ("G", a + 1)]
-        steps += [("M", a + 2), ("R", a + 2), ("A", a + 2), ("A", a + 1), ("M", a + 3), ("R", a + 3), ("A", a + 3)]
+        a = n_units - 6
+        steps += [("M", a), ("M", a + 1), ("R", a), ("A", a), ("G", a + 1), ("M", a + 2), ("G", a + 2), ("A", a + 1)]
+        steps += [("M", a + 3), ("M", a + 4), ("R", a + 3), ("A", a + 2), ("A", a + 3)]
+        steps += [("M", a + 5), ("R", a + 4), ("A", a + 4), ("R", a + 5), ("A", a + 5)]
 
         accs = []
         for i in range(BANKS):

@@ -241,8 +241,11 @@ def tile_linearattention_pa_kernel(
             accs.append(acc)
         for i in range(WARM_MATMULS):
             nc.tensor.matmul(out=accs[BANKS - 1][:], lhsT=zz[:, 0:P], rhs=zz[:], start=True, stop=True)
-        for g in range(PASSES):
+        for g in range(PASSES - 2):
             for i in ((0, 2, 4, 6, 1, 3, 5, 7) if g == 0 else range(BANKS)):
+                one_pass(accs[i], units[i], g)
+        for i in range(BANKS):
+            for g in range(PASSES - 2, PASSES):
                 one_pass(accs[i], units[i], g)
         for kind, k in steps:
             if kind == "M":

@@ -146,8 +146,7 @@ def tile_linearattention_pa_kernel(
         zs = keep.tile([P, TOKEN_TILES, PAIRS], F32, name="zs")
         gq = keep.tile([P, TOKEN_TILES, PAIRS], F32, name="gq")
         zc = keep.tile([P, TOKEN_TILES, PAIRS], F32, name="zc")
-        sin_t = keep.tile([P, TOKEN_TILES, 2, PAIRS], F32, name="sin_t")
-        cos_t = keep.tile([P, TOKEN_TILES, PAIRS], F32, name="cos_t")
+        tab = keep.tile([P, TOKEN_TILES, 4, PAIRS], F32, name="tab")
         nc.vector.tensor_copy(out=whole[:], in_=t1[:])
         nc.vector.tensor_tensor(out=frac[:], in0=t1[:], in1=whole[:], op=ALU.subtract)
         nc.vector.tensor_tensor(out=frac[:, :, 0:SPLIT_PAIRS], in0=frac[:, :, 0:SPLIT_PAIRS], in1=t2[:], op=ALU.add)
@@ -155,9 +154,10 @@ def tile_linearattention_pa_kernel(
         nc.vector.tensor_scalar(out=gq[:], in0=frac[:], scalar1=0.25, scalar2=None, op0=ALU.add)
         nc.vector.scalar_tensor_tensor(out=zs[:], in0=z1[:], scalar=0.5, in1=z1[:], op0=ALU.is_gt, op1=ALU.subtract)
         nc.vector.scalar_tensor_tensor(out=zc[:], in0=gq[:], scalar=0.5, in1=gq[:], op0=ALU.is_gt, op1=ALU.subtract)
-        nc.scalar.activation(out=sin_t[:, :, 0, :], in_=zs[:], func=ACTF.Sin, scale=TWO_PI)
-        nc.scalar.activation(out=sin_t[:, :, 1, :], in_=zs[:], func=ACTF.Sin, scale=-TWO_PI)
-        nc.scalar.activation(out=cos_t[:], in_=zc[:], func=ACTF.Sin, scale=-TWO_PI)
+        nc.scalar.activation(out=tab[:, :, 2, :], in_=zs[:], func=ACTF.Sin, scale=TWO_PI)
+        nc.scalar.activation(out=tab[:, :, 3, :], in_=zs[:], func=ACTF.Sin, scale=-TWO_PI)
+        nc.scalar.activation(out=tab[:, :, 0, :], in_=zc[:], func=ACTF.Sin, scale=-TWO_PI)
+        nc.scalar.activation(out=tab[:, :, 1, :], in_=zc[:], func=ACTF.Sin, scale=-TWO_PI)
         make_planes("x2", 0, 8)
         make_planes("x3", 0, 8)
 
@@ -183,23 +183,26 @@ def tile_linearattention_pa_kernel(
 
         def multiply(i):
             t, wn, c0, n = units[i]
-            shape = [P, 2, n // DH, PAIRS]
+            shape = [P, 2, 2, n // DH, PAIRS]
             u = accs[i][:].rearrange("p (h j e) -> p e h j", h=n // DH, j=PAIRS, e=2)
-            uc = ep.tile(shape, F32, name="uc")
-            us = ep.tile(shape, F32, name="us")
-            nc.vector.tensor_tensor(out=uc[:], in0=u, in1=cos_t[:, t, :].unsqueeze(1).unsqueeze(1).to_broadcast(shape), op=ALU.mult)
-            nc.vector.tensor_tensor(out=us[:], in0=u, in1=sin_t[:, t, :, :].unsqueeze(2).to_broadcast(shape), op=ALU.mult)
-            held[i] = (uc, us)
+            prod = ep.tile(shape, F32, name="prod")
+            nc.vector.tensor_tensor(
+                out=prod[:],
+                in0=u.unsqueeze(1).to_broadcast(shape),
+                in1=tab[:, t, :, :].rearrange("p (c e) j -> p c e j", c=2).unsqueeze(3).to_broadcast(shape),
+                op=ALU.mult,
+            )
+            held[i] = prod
 
         def rotate(i, on_gpsimd):
             n = units[i][3]
-            uc, us = held[i]
+            prod = held[i]
             rot = ep.tile([P, 2, n // DH, PAIRS], F32, name="rot")
             if on_gpsimd:
-                nc.gpsimd.tensor_tensor(out=rot[:, 0], in0=uc[:, 0], in1=us[:, 1], op=ALU.add)
-                nc.gpsimd.tensor_tensor(out=rot[:, 1], in0=uc[:, 1], in1=us[:, 0], op=ALU.add)
+                nc.gpsimd.tensor_tensor(out=rot[:, 0], in0=prod[:, 0, 0], in1=prod[:, 1, 1], op=ALU.add)
+                nc.gpsimd.tensor_tensor(out=rot[:, 1], in0=prod[:, 0, 1], in1=prod[:, 1, 0], op=ALU.add)
             else:
-                nc.vector.tensor_tensor(out=rot[:], in0=uc[:], in1=us[:, ::-1], op=ALU.add)
+                nc.vector.tensor_tensor(out=rot[:], in0=prod[:, 0], in1=prod[:, 1, ::-1], op=ALU.add)
             held[i] = rot
 
         def relu_store(i):

@@ -205,12 +205,15 @@ def tile_linearattention_pa_kernel(
                 nc.vector.tensor_tensor(out=rot[:], in0=prod[:, 0], in1=prod[:, 1, ::-1], op=ALU.add)
             held[i] = rot
 
-        def relu_store(i):
+        def relu_store(i, on_vector):
             t, wn, c0, n = units[i]
             nh = n // DH
             rot = held[i]
             res = ep.tile([P, nh, PAIRS, 2], F32, name="res", bufs=6)
-            nc.scalar.activation(out=res[:], in_=rot[:].rearrange("p e h j -> p h j e"), func=ACTF.Relu)
+            if on_vector:
+                nc.vector.tensor_scalar(out=res[:], in0=rot[:].rearrange("p e h j -> p h j e"), scalar1=0.0, scalar2=None, op0=ALU.max)
+            else:
+                nc.scalar.activation(out=res[:], in_=rot[:].rearrange("p e h j -> p h j e"), func=ACTF.Relu)
             dst = out_0 if wn == "wq" else out_1
             h0 = c0 // DH
             nc.sync.dma_start(
@@ -236,7 +239,7 @@ def tile_linearattention_pa_kernel(
         a = n_units - 6
         steps += [("M", a), ("M", a + 1), ("R", a), ("A", a), ("G", a + 1), ("M", a + 2), ("G", a + 2), ("A", a + 1)]
         steps += [("M", a + 3), ("M", a + 4), ("R", a + 3), ("A", a + 2), ("A", a + 3)]
-        steps += [("M", a + 5), ("R", a + 4), ("A", a + 4), ("R", a + 5), ("A", a + 5)]
+        steps += [("M", a + 5), ("R", a + 4), ("R", a + 5), ("X", a + 4), ("X", a + 5)]
 
         accs = []
         for i in range(BANKS):
@@ -267,7 +270,7 @@ def tile_linearattention_pa_kernel(
                     accs.append(acc)
                     for g in range(PASSES):
                         one_pass(acc, units[i], g)
-            elif kind == "A":
-                relu_store(k)
+            elif kind in ("A", "X"):
+                relu_store(k, kind == "X")
             else:
                 rotate(k, kind == "G")

from contextlib import ExitStack

import concourse.mybir as mybir

FLOPS = 2 * 2048 * 4096 * 2048

F32 = mybir.dt.float32
I32 = mybir.dt.int32
U8 = mybir.dt.uint8
BF16 = mybir.dt.bfloat16
FP4X4 = mybir.dt.float4_e2m1fn_x4
ALU = mybir.AluOpType
ACTF = mybir.ActivationFunctionType

P = 128
PASSES = 8
N_TILE = 512
TOKEN_TILES = 16
PAIRS = 64
DH = 128
TWO_PI = 6.283185307179586
ROPE_BASE = 10000.0
SPLIT_PAIRS = 32
HI_BITS = 13
BANKS = 8
WARM_MATMULS = 8
LAG_UNTIL = 40


def split_hi_lo(value):
    shift = 0
    while value * 2.0**shift < 2.0 ** (HI_BITS - 1):
        shift += 1
    hi = round(value * 2.0**shift) / 2.0**shift
    return hi, value - hi


def tile_linearattention_pa_kernel(
    tc, x_words, x_scales, wq_words, wq_scales, wk_words, wk_scales, out_0, out_1
):
    nc = tc.nc
    parts = {
        "x0": (x_words, x_scales, 0, 512),
        "x1": (x_words, x_scales, 512, 1024),
        "x2": (x_words, x_scales, 1024, 1536),
        "x3": (x_words, x_scales, 1536, 2048),
        "wq": (wq_words, wq_scales, 0, 1024),
        "wk": (wk_words, wk_scales, 0, 1024),
    }

    with ExitStack() as ctx:
        keep = ctx.enter_context(tc.tile_pool(name="keep", bufs=1))
        ep = ctx.enter_context(tc.tile_pool(name="ep", bufs=4))
        psum = ctx.enter_context(tc.psum_pool(name="psum", bufs=BANKS))
        ctx.enter_context(tc.manual_schedule())

        codes = {}
        planes = {}

        def make_planes(name, g0, g1):
            c0, c1 = parts[name][2], parts[name][3]
            t = keep.tile([P, g1 - g0, c1 - c0], U8, name="%s_p%d" % (name, g0), align_bytes=256)
            nc.vector.memset(t[:].bitcast(I32), 0)
            for g in range(g0, g1):
                planes[(name, g)] = (t, g - g0)

        def load_scales(name, g0, g1):
            scales, c0, c1 = parts[name][1], parts[name][2], parts[name][3]
            t = planes[(name, g0)][0]
            for q in (0, 2, 1, 3):
                nc.sync.dma_start(
                    out=t[32 * q : 32 * q + 4, :, :].bitcast(I32),
                    in_=scales[g0:g1, 4 * q : 4 * q + 4, c0:c1].rearrange("g r n -> r g n").bitcast(I32),
                )

        def load_codes(name, g0, g1, lo=0, hi=None):
            words, c0 = parts[name][0], parts[name][2]
            hi = parts[name][3] - c0 if hi is None else hi
            t = keep.tile([P, g1 - g0, 2 * (hi - lo)], U8, name="%s_c%d_%d" % (name, g0, lo), align_bytes=256)
            nc.sync.dma_start(
                out=t[:].bitcast(I32),
                in_=words[g0:g1, :, 2 * (c0 + lo) : 2 * (c0 + hi)].rearrange("g p n -> p g n").bitcast(I32),
            )
            for g in range(g0, g1):
                codes.setdefault((name, g), []).append((t, g - g0, lo, hi))

        def find_codes(name, g, lo, hi):
            for t, slot, a, b in codes[(name, g)]:
                if a <= lo and hi <= b:
                    return t, slot, lo - a
            return None

        pos = keep.tile([P, TOKEN_TILES], F32, name="pos")
        nc.gpsimd.iota(pos[:], pattern=[[P, TOKEN_TILES]], base=0, channel_multiplier=1, allow_small_or_imprecise_dtypes=True)

        zz = keep.tile([P, N_TILE], BF16, name="zz")
        nc.vector.memset(zz[:], 0.0)
        make_planes("wq", 0, 2)
        make_planes("x0", 0, 2)
        make_planes("x0", 2, 8)
        make_planes("wq", 2, 5)
        make_planes("wq", 5, 8)

        load_codes("x0", 0, 1)
        load_codes("wq", 0, 1, 0, 512)
        load_scales("wq", 0, 2)
        load_scales("x0", 0, 2)
        load_codes("wq", 0, 1, 512, 1024)
        load_codes("x0", 1, 2)
        load_codes("wq", 1, 2)
        load_scales("x0", 2, 8)
        load_scales("wq", 2, 5)
        for g in range(2, 4):
            load_codes("x0", g, g + 1)
            load_codes("wq", g, g + 1)
        load_scales("wq", 5, 8)
        for g in range(4, 8):
            load_codes("x0", g, g + 1)
            load_codes("wq", g, g + 1)

        warm = keep.tile([P, 1], F32, name="warm")
        nc.scalar.activation(out=warm[:], in_=pos[:, 0:1], func=ACTF.Sin, scale=0.0)
        t1 = keep.tile([P, TOKEN_TILES, PAIRS], F32, name="t1")
        t2 = keep.tile([P, TOKEN_TILES, SPLIT_PAIRS], F32, name="t2")
        for j in range(PAIRS):
            turns = ROPE_BASE ** (-j / 64.0) / TWO_PI
            if j < SPLIT_PAIRS:
                hi, lo = split_hi_lo(turns)
                nc.vector.tensor_scalar(out=t1[:, :, j], in0=pos[:], scalar1=hi, scalar2=None, op0=ALU.mult)
                nc.scalar.activation(out=t2[:, :, j], in_=pos[:], func=ACTF.Copy, scale=lo)
            else:
                nc.scalar.activation(out=t1[:, :, j], in_=pos[:], func=ACTF.Copy, scale=turns)

        make_planes("x1", 0, 8)
        make_planes("wk", 0, 8)
        load_scales("x1", 0, 8)
        load_codes("x1", 0, 4)
        load_codes("x1", 4, 8)
        load_scales("wk", 0, 8)
        for g in range(0, 8, 2):
            load_codes("wk", g, g + 2)

        whole = keep.tile([P, TOKEN_TILES, PAIRS], I32, name="whole")
        frac = keep.tile([P, TOKEN_TILES, PAIRS], F32, name="frac")
        z1 = keep.tile([P, TOKEN_TILES, PAIRS], F32, name="z1")
        zs = keep.tile([P, TOKEN_TILES, PAIRS], F32, name="zs")
        gq = keep.tile([P, TOKEN_TILES, PAIRS], F32, name="gq")
        zc = keep.tile([P, TOKEN_TILES, PAIRS], F32, name="zc")
        tab = keep.tile([P, TOKEN_TILES, 4, PAIRS], F32, name="tab")
        nc.vector.tensor_copy(out=whole[:], in_=t1[:])
        nc.vector.tensor_tensor(out=frac[:], in0=t1[:], in1=whole[:], op=ALU.subtract)
        nc.vector.tensor_tensor(out=frac[:, :, 0:SPLIT_PAIRS], in0=frac[:, :, 0:SPLIT_PAIRS], in1=t2[:], op=ALU.add)
        nc.vector.scalar_tensor_tensor(out=z1[:], in0=frac[:], scalar=0.5, in1=frac[:], op0=ALU.is_gt, op1=ALU.subtract)
        nc.vector.tensor_scalar(out=gq[:], in0=frac[:], scalar1=0.25, scalar2=None, op0=ALU.add)
        nc.vector.scalar_tensor_tensor(out=zs[:], in0=z1[:], scalar=0.5, in1=z1[:], op0=ALU.is_gt, op1=ALU.subtract)
        nc.vector.scalar_tensor_tensor(out=zc[:], in0=gq[:], scalar=0.5, in1=gq[:], op0=ALU.is_gt, op1=ALU.subtract)
        nc.scalar.activation(out=tab[:, :, 2, :], in_=zs[:], func=ACTF.Sin, scale=TWO_PI)
        nc.scalar.activation(out=tab[:, :, 3, :], in_=zs[:], func=ACTF.Sin, scale=-TWO_PI)
        nc.scalar.activation(out=tab[:, :, 0, :], in_=zc[:], func=ACTF.Sin, scale=-TWO_PI)
        nc.scalar.activation(out=tab[:, :, 1, :], in_=zc[:], func=ACTF.Sin, scale=-TWO_PI)
        make_planes("x2", 0, 8)
        make_planes("x3", 0, 8)

        def one_pass(acc, unit, g):
            t, wn, c0, n = unit
            xn = "x%d" % (t // 4)
            tl = t % 4
            xc, xci, xo = find_codes(xn, g, P * tl, P * (tl + 1))
            wc, wci, wo = find_codes(wn, g, c0, c0 + n)
            xp, xpi = planes[(xn, g)]
            wp, wpi = planes[(wn, g)]
            nc.tensor.matmul_mx(
                out=acc[:],
                lhsT=xc[:, xci, 2 * xo : 2 * (xo + P)].bitcast(FP4X4),
                lhsT_scale=xp[:, xpi, P * tl : P * (tl + 1)],
                rhs=wc[:, wci, 2 * wo : 2 * (wo + n)].bitcast(FP4X4),
                rhs_scale=wp[:, wpi, c0 : c0 + n],
                start=(g == 0),
                stop=(g == PASSES - 1),
            )

        held = {}

        def multiply(i):
            t, wn, c0, n = units[i]
            shape = [P, 2, 2, n // DH, PAIRS]
            u = accs[i][:].rearrange("p (h j e) -> p e h j", h=n // DH, j=PAIRS, e=2)
            prod = ep.tile(shape, F32, name="prod")
            nc.vector.tensor_tensor(
                out=prod[:],
                in0=u.unsqueeze(1).to_broadcast(shape),
                in1=tab[:, t, :, :].rearrange("p (c e) j -> p c e j", c=2).unsqueeze(3).to_broadcast(shape),
                op=ALU.mult,
            )
            held[i] = prod

        def rotate(i, on_gpsimd):
            n = units[i][3]
            prod = held[i]
            rot = ep.tile([P, 2, n // DH, PAIRS], F32, name="rot")
            if on_gpsimd:
                nc.gpsimd.tensor_tensor(out=rot[:, 0], in0=prod[:, 0, 0], in1=prod[:, 1, 1], op=ALU.add)
                nc.gpsimd.tensor_tensor(out=rot[:, 1], in0=prod[:, 0, 1], in1=prod[:, 1, 0], op=ALU.add)
            else:
                nc.vector.tensor_tensor(out=rot[:], in0=prod[:, 0], in1=prod[:, 1, ::-1], op=ALU.add)
            held[i] = rot

        def relu_store(i, on_vector):
            t, wn, c0, n = units[i]
            nh = n // DH
            rot = held[i]
            res = ep.tile([P, nh, PAIRS, 2], F32, name="res", bufs=6)
            if on_vector:
                nc.vector.tensor_scalar(out=res[:], in0=rot[:].rearrange("p e h j -> p h j e"), scalar1=0.0, scalar2=None, op0=ALU.max)
            else:
                nc.scalar.activation(out=res[:], in_=rot[:].rearrange("p e h j -> p h j e"), func=ACTF.Relu)
            dst = out_0 if wn == "wq" else out_1
            h0 = c0 // DH
            nc.sync.dma_start(
                out=dst[0, h0 : h0 + nh, P * t : P * (t + 1), :].rearrange("h p d -> p h d"),
                in_=res[:].rearrange("p h j e -> p h (j e)"),
            )

        units = [(t, "wq", c0, N_TILE) for t in range(0, 8) for c0 in (0, 512)]
        units += [(t, "wk", c0, N_TILE) for t in range(0, 8) for c0 in (0, 512)]
        units += [(t, wn, c0, N_TILE) for t in range(8, TOKEN_TILES) for wn in ("wq", "wk") for c0 in (0, 512)]
        units = units[:-2]
        units += [(TOKEN_TILES - 1, "wk", c0, n) for c0, n in ((0, 256), (256, 256), (512, 256), (768, 128), (896, 128))]
        n_units = len(units)

        steps = []
        for k in range(LAG_UNTIL):
            steps.append(("M", k))
            if k > 0:
                steps += [("R", k - 1), ("A", k - 1)]
        steps += [("R", LAG_UNTIL - 1), ("A", LAG_UNTIL - 1)]
        for k in range(LAG_UNTIL, n_units - 6):
            steps += [("M", k), ("R", k), ("A", k)]
        a = n_units - 6
        steps += [("M", a), ("M", a + 1), ("R", a), ("A", a), ("G", a + 1), ("M", a + 2), ("G", a + 2), ("A", a + 1)]
        steps += [("M", a + 3), ("M", a + 4), ("R", a + 3), ("A", a + 2), ("A", a + 3)]
        steps += [("M", a + 5), ("R", a + 4), ("R", a + 5), ("X", a + 4), ("X", a + 5)]

        accs = []
        for i in range(BANKS):
            acc = psum.tile([P, N_TILE], F32, name="acc")
            accs.append(acc)
        for i in range(WARM_MATMULS):
            nc.tensor.matmul(out=accs[BANKS - 1][:], lhsT=zz[:, 0:P], rhs=zz[:], start=True, stop=True)
        for g in range(PASSES - 2):
            for i in ((0, 2, 4, 6, 1, 3, 5, 7) if g == 0 else range(BANKS)):
                one_pass(accs[i], units[i], g)
        for i in range(BANKS):
            for g in range(PASSES - 2, PASSES):
                one_pass(accs[i], units[i], g)
        for kind, k in steps:
            if kind == "M":
                multiply(k)
                i = k + BANKS
                if i == 16:
                    load_scales("x2", 0, 8)
                    load_codes("x2", 0, 4)
                    load_codes("x2", 4, 8)
                if i == 32:
                    load_scales("x3", 0, 8)
                    load_codes("x3", 0, 4)
                    load_codes("x3", 4, 8)
                if i < n_units:
                    acc = psum.tile([P, units[i][3]], F32, name="acc")
                    accs.append(acc)
                    for g in range(PASSES):
                        one_pass(acc, units[i], g)
            elif kind in ("A", "X"):
                relu_store(k, kind == "X")
            else:
                rotate(k, kind == "G")
